import numpy as np
import ml_dtypes


def mxq(x, axis, fmt="e4m3"):
    dtype, down = {"e4m3": (ml_dtypes.float8_e4m3fn, 7), "e5m2": (ml_dtypes.float8_e5m2, 14)}[fmt]
    v = np.moveaxis(np.asarray(x, np.float32).astype(ml_dtypes.bfloat16).astype(np.float64), axis, -1)
    blocks = v.reshape(v.shape[:-1] + (-1, 32))
    amax = np.abs(blocks).max(-1, keepdims=True)
    byte = np.maximum(np.where(amax > 0, np.frexp(amax)[1] - 1 + 127, 0) - down, 1)
    scale = np.exp2(byte - 127.0)
    codes = (blocks / scale).astype(np.float32).astype(dtype).astype(np.float64)
    return np.moveaxis((codes * scale).reshape(v.shape), -1, axis)


WIDE = False


def mx_kscale(k):
    if not WIDE:
        return np.ones(k)
    levels = np.array([10, -10, 5, -5, 0])
    if k % 512:
        return np.exp2(np.random.permutation(np.resize(levels, k // 32))).repeat(32)
    a = np.empty((k // 512, 16))
    for p in range(k // 512):
        a[p, :8] = np.random.permutation(np.resize(levels, 8))
        for g in range(8):
            far = levels[np.abs(levels - a[p, g]) >= 10]
            a[p, g + 8] = far[np.random.randint(len(far))]
    return np.exp2(a.ravel()).repeat(32)


BF16 = ml_dtypes.bfloat16


def bf(x):
    return np.asarray(x, np.float32).astype(BF16)


def f64(x):
    return np.asarray(x).astype(np.float64)


B, S, H, NH, NKV, HD = 2, 256, 2048, 16, 4, 128
ROPE_THETA = 10000.0


def rope_tables():
    inv_freq = 1.0 / (ROPE_THETA ** (np.arange(0, HD, 2) / HD))
    pos = np.arange(S)[None, :] + np.random.randint(0, S, (B, 1))
    freqs = pos[:, :, None] * inv_freq[None, None, :]
    emb = np.concatenate([freqs, freqs], axis=-1)
    return np.cos(emb), np.sin(emb)


def rotate_half(x):
    x1, x2 = np.split(x, 2, axis=-1)
    return np.concatenate([-x2, x1], axis=-1)


def draw0():
    s = mx_kscale(H)
    hidden_states = bf(np.random.standard_normal((B, S, H)) * s)
    q_w = bf(np.random.standard_normal((NH * HD, H)) / np.sqrt(H) / s[None, :])
    k_w = bf(np.random.standard_normal((NKV * HD, H)) / np.sqrt(H) / s[None, :])
    v_w = bf(np.random.standard_normal((NKV * HD, H)) / np.sqrt(H) / s[None, :])
    cos, sin = rope_tables()
    return {"hidden_states": hidden_states, "cos": bf(cos), "sin": bf(sin), "q_w": q_w, "k_w": k_w, "v_w": v_w}


def core(hidden_states, cos, sin, q_w, k_w, v_w):
    b, s, _ = hidden_states.shape
    xq = mxq(f64(hidden_states), 2, "e4m3")
    q = (xq @ mxq(f64(q_w), 1, "e4m3").T).reshape(b, s, NH, HD).transpose(0, 2, 1, 3)
    k = (xq @ mxq(f64(k_w), 1, "e4m3").T).reshape(b, s, NKV, HD).transpose(0, 2, 1, 3)
    v = (xq @ mxq(f64(v_w), 1, "e4m3").T).reshape(b, s, NKV, HD).transpose(0, 2, 1, 3)
    c = f64(cos)[:, None, :, :]
    sn = f64(sin)[:, None, :, :]
    q = q * c + rotate_half(q) * sn
    k = k * c + rotate_half(k) * sn
    return (q, k, v)


def e4m3fn_bytes(y):
    return np.clip(np.asarray(y, np.float64), -448.0, 448.0).astype(np.float32).astype(ml_dtypes.float8_e4m3fn).view(np.uint8)


def e4m3fn_values(b):
    return np.asarray(b, np.uint8).view(ml_dtypes.float8_e4m3fn).astype(np.float64)


def setup_inputs():
    d = draw0()
    x0 = np.asarray(d['q_w']).astype(np.float64)
    s = (np.max(np.abs(x0), axis=(0,), keepdims=True) / 448.0).astype(np.float32)
    out = {}
    for k, v in d.items():
        if k == 'q_w':
            out['q_w_bytes'] = e4m3fn_bytes(x0 / s.astype(np.float64))
            out['q_w_scale'] = s
        else:
            out[k] = v
    return out


def reference(hidden_states, cos, sin, q_w_bytes, q_w_scale, k_w, v_w):
    return core(hidden_states, cos, sin, e4m3fn_values(q_w_bytes) * q_w_scale.astype(np.float64), k_w, v_w)

@@ -1,0 +1,399 @@
+from contextlib import ExitStack
+
+import concourse.mybir as mybir
+from concourse.masks import make_identity
+
+FLOPS = 2 * 512 * 2048 * 3072
+
+F32 = mybir.dt.float32
+BF16 = mybir.dt.bfloat16
+U8 = mybir.dt.uint8
+U32 = mybir.dt.uint32
+FP8 = mybir.dt.float8_e4m3fn
+FP8X4 = mybir.dt.float8_e4m3fn_x4
+MULT = mybir.AluOpType.mult
+ADD = mybir.AluOpType.add
+
+P = 128
+K = 2048
+PASSES = 4
+PASS_K = K // PASSES
+PACK = 4
+GROUP = 512
+HEADS = GROUP // P
+HALF = P // 2
+TOKEN_TILES = 4
+PSUM_BANKS = 8
+SCALE_SLOT = 8
+TURNS_AHEAD = 3
+
+
+def tile_mistralattention_kernel(
+    tc, hidden_states, cos, sin, q_w_bytes, q_w_scale, k_w, v_w, out_0, out_1, out_2
+):
+    nc = tc.nc
+    rows_of = {"x": hidden_states.flatten_outer_dims(), "k": k_w, "v": v_w}
+
+    with ExitStack() as ctx:
+        const = ctx.enter_context(tc.tile_pool(name="const", bufs=1))
+        bytes_pool = ctx.enter_context(tc.tile_pool(name="bytes", bufs=16))
+        rows_pool = ctx.enter_context(tc.tile_pool(name="rows", bufs=8))
+        scaled_pool = ctx.enter_context(tc.tile_pool(name="scaled", bufs=4))
+        widened_pool = ctx.enter_context(tc.tile_pool(name="widened", bufs=4))
+        grouped_pool = ctx.enter_context(tc.tile_pool(name="grouped", bufs=3))
+        codes_pool = ctx.enter_context(tc.tile_pool(name="codes", bufs=3))
+        cos_part_pool = ctx.enter_context(tc.tile_pool(name="cos_part", bufs=3))
+        sin_part_pool = ctx.enter_context(tc.tile_pool(name="sin_part", bufs=3))
+        plain_pool = ctx.enter_context(tc.tile_pool(name="plain", bufs=2))
+        psum = ctx.enter_context(tc.psum_pool(name="psum", bufs=1))
+        ctx.enter_context(tc.manual_schedule())
+
+        ident = const.tile([P, P], F32, name="ident")
+        scale_on_rows = const.tile([P, K], F32, name="scale_on_rows")
+        scale_on_k = const.tile([P, PASSES, SCALE_SLOT], F32, name="scale_on_k")
+        cos_sb = const.tile([P, TOKEN_TILES, P], BF16, name="cos_sb")
+        sin_sb = const.tile([P, TOKEN_TILES, P], BF16, name="sin_sb")
+        signed_sin = const.tile([P, TOKEN_TILES, P], BF16, name="signed_sin")
+        x_codes = const.tile([P, PASSES * GROUP], U32, name="x_codes", align_bytes=64)
+        x_scales = const.tile([P, PASSES * GROUP], U8, name="x_scales", align_bytes=64)
+
+        q_bytes = {}
+        row_tiles = {}
+        needs_scale = {}
+        turned = {}
+        grouped = {}
+        codes = {"x": x_codes}
+        scales = {"x": x_scales}
+        sums = {}
+        parts = {}
+
+        free_banks = list(range(PSUM_BANKS))
+
+        def take_bank():
+            b = free_banks[0]
+            free_banks.remove(b)
+            t = psum.tile([P, GROUP], F32, name="bank%d" % b, tag="bank%d" % b)
+            return (b, t)
+
+        def load_bytes(j, r):
+            t = bytes_pool.tile([P, K], U8, name="q_bytes", tag="q_bytes")
+            row0 = GROUP * j + P * r
+            nc.sync.dma_start(out=t[:], in_=q_w_bytes[row0 : row0 + P, :])
+            q_bytes[(j, r)] = t
+
+        def load_rows(grp, r):
+            t = rows_pool.tile([P, K], BF16, name="rows", tag="rows")
+            nc.sync.dma_start(out=t[:], in_=rows_of[grp][P * r : P * (r + 1), :])
+            row_tiles[(grp, r)] = t
+            needs_scale[(grp, r)] = False
+
+        def load_scale_on_k(g):
+            nc.sync.dma_start(
+                out=scale_on_k[:, g, 0:PACK],
+                in_=q_w_scale.rearrange("o (g p t) -> g p (o t)", p=P, t=PACK)[g],
+            )
+
+        def load_tables():
+            nc.sync.dma_start(out=cos_sb[:], in_=cos.rearrange("b (t s) d -> s (b t) d", s=P))
+            nc.sync.dma_start(out=sin_sb[:], in_=sin.rearrange("b (t s) d -> s (b t) d", s=P))
+            nc.gpsimd.tensor_scalar(
+                out=signed_sin[:, :, 0:HALF],
+                in0=sin_sb[:, :, 0:HALF],
+                scalar1=-1.0,
+                scalar2=None,
+                op0=MULT,
+            )
+            nc.gpsimd.tensor_copy(out=signed_sin[:, :, HALF:P], in_=sin_sb[:, :, HALF:P])
+
+        def spread_scale(g):
+            b, bank = take_bank()
+            for t in range(PACK):
+                column = scale_on_k[:, g, t : t + 1]
+                nc.tensor.transpose(bank[:, P * t : P * (t + 1)], column.to_broadcast([P, P]), ident[:])
+            free_banks.append(b)
+            nc.scalar.copy(
+                out=scale_on_rows[:, PASS_K * g : PASS_K * (g + 1)].rearrange("p (n t) -> p n t", t=PACK),
+                in_=bank[:].rearrange("p (t n) -> p n t", t=PACK),
+            )
+
+        def scale_rows(j, r, pieces=1):
+            t = scaled_pool.tile([P, K], BF16, name="scaled", tag="scaled")
+            width = K // pieces
+            for c in range(pieces):
+                cols = slice(width * c, width * (c + 1))
+                nc.vector.tensor_tensor(
+                    out=t[:, cols],
+                    in0=q_bytes[(j, r)][:, cols].bitcast(FP8),
+                    in1=scale_on_rows[:, cols],
+                    op=MULT,
+                )
+            row_tiles[(j, r)] = t
+            needs_scale[(j, r)] = False
+
+        def widen_rows(j, r):
+            t = widened_pool.tile([P, K], BF16, name="widened", tag="widened")
+            nc.scalar.copy(out=t[:], in_=q_bytes[(j, r)][:].bitcast(FP8))
+            row_tiles[(j, r)] = t
+            needs_scale[(j, r)] = True
+
+        def turn(grp, a, g):
+            b, bank = take_bank()
+            for u in range(2):
+                for half_pair in range(2):
+                    words = row_tiles[(grp, 2 * a + half_pair)][:].bitcast(F32)
+                    c0 = (2 * u + half_pair) * P
+                    nc.tensor.transpose(
+                        bank[:, c0 : c0 + P], words[:, 256 * g + u : 256 * (g + 1) : 2], ident[:]
+                    )
+            turned[(grp, a, g)] = (b, bank)
+
+        def empty(grp, a, g):
+            if grp not in grouped:
+                gt = grouped_pool.tile(
+                    [P, PASSES * GROUP * PACK], BF16, name="grouped", tag="grouped", align_bytes=64
+                )
+                grouped[grp] = gt
+            b, bank = turned[(grp, a, g)]
+            free_banks.append(b)
+            c0 = GROUP * PACK * g + 2 * P * PACK * a
+            dst = grouped[grp][:, c0 : c0 + 2 * P * PACK]
+            if needs_scale[(grp, 2 * a)]:
+                nc.vector.tensor_tensor(
+                    out=dst.rearrange("p (r u e) -> p r u e", u=2, e=2),
+                    in0=bank[:].bitcast(BF16).rearrange("p (u r e) -> p r u e", u=2, e=2),
+                    in1=scale_on_k[:, g, 0:PACK]
+                    .rearrange("p (o u e) -> p o u e", o=1, u=2)
+                    .to_broadcast([P, 2 * P, 2, 2]),
+                    op=MULT,
+                )
+            else:
+                nc.scalar.copy(
+                    out=dst.bitcast(F32).rearrange("p (r u) -> p r u", u=2),
+                    in_=bank[:].rearrange("p (u r) -> p r u", u=2),
+                )
+
+        def turn_and_empty(grp, a, passes):
+            for g in passes:
+                turn(grp, a, g)
+                empty(grp, a, g)
+
+        def quantize(grp, h):
+            if h == 0 and grp != "x":
+                ct = codes_pool.tile([P, PASSES * GROUP], U32, name="codes", tag="codes", align_bytes=64)
+                st = codes_pool.tile([P, PASSES * GROUP], U8, name="scales", tag="scales", align_bytes=64)
+                codes[grp] = ct
+                scales[grp] = st
+            cols = slice(2 * GROUP * h, 2 * GROUP * (h + 1))
+            nc.vector.quantize_mx(
+                out=codes[grp][:, cols].bitcast(FP8X4),
+                scales=scales[grp][:, cols],
+                in_=grouped[grp][:, 2 * GROUP * PACK * h : 2 * GROUP * PACK * (h + 1)],
+            )
+
+        def project(grp, m):
+            b, bank = take_bank()
+            for g in range(PASSES):
+                x_cols = slice(GROUP * g + P * m, GROUP * g + P * (m + 1))
+                w_cols = slice(GROUP * g, GROUP * (g + 1))
+                nc.tensor.matmul_mx(
+                    out=bank[:],
+                    lhsT=x_codes[:, x_cols].bitcast(FP8X4),
+                    lhsT_scale=x_scales[:, x_cols],
+                    rhs=codes[grp][:, w_cols].bitcast(FP8X4),
+                    rhs_scale=scales[grp][:, w_cols],
+                    start=(g == 0),
+                    stop=(g == PASSES - 1),
+                )
+            sums[(grp, m)] = (b, bank)
+
+        def dest(grp, m):
+            batch = m // 2
+            s0 = P * (m % 2)
+            if grp == "k":
+                o = out_1[batch, :, s0 : s0 + P, :]
+            elif grp == "v":
+                o = out_2[batch, :, s0 : s0 + P, :]
+            else:
+                o = out_0[batch, HEADS * grp : HEADS * (grp + 1), s0 : s0 + P, :]
+            return o.rearrange("h s d -> s h d")
+
+        def rope_products(grp, m):
+            if m % 2 == 0:
+                ct = cos_part_pool.tile([P, 2 * GROUP], F32, name="cos_part", tag="cos_part")
+                st = sin_part_pool.tile([P, 2 * GROUP], F32, name="sin_part", tag="sin_part")
+                parts[(grp, m // 2)] = (ct, st)
+            cos_part, sin_part = parts[(grp, m // 2)]
+            cols = slice(GROUP * (m % 2), GROUP * (m % 2 + 1))
+            b, bank = sums[(grp, m)]
+            free_banks.append(b)
+            nc.vector.tensor_tensor(
+                out=cos_part[:, cols].rearrange("p (h d) -> p h d", h=HEADS),
+                in0=bank[:].rearrange("p (h d) -> p h d", h=HEADS),
+                in1=cos_sb[:, m : m + 1, :].to_broadcast([P, HEADS, P]),
+                op=MULT,
+            )
+            nc.vector.tensor_tensor(
+                out=sin_part[:, cols].rearrange("p (h f j) -> p h f j", h=HEADS, f=2),
+                in0=bank[:].rearrange("p (h f j) -> p h f j", h=HEADS, f=2)[:, :, ::-1, :],
+                in1=signed_sin[:, m, :]
+                .rearrange("p (o f j) -> p o f j", o=1, f=2)
+                .to_broadcast([P, HEADS, 2, HALF]),
+                op=MULT,
+            )
+
+        def rope_sum(engine, grp, ms):
+            cos_part, sin_part = parts[(grp, ms[0] // 2)]
+            cols = slice(GROUP * (ms[0] % 2), GROUP * (ms[-1] % 2 + 1))
+            engine.tensor_tensor(out=cos_part[:, cols], in0=cos_part[:, cols], in1=sin_part[:, cols], op=ADD)
+            for m in ms:
+                m_cols = slice(GROUP * (m % 2), GROUP * (m % 2 + 1))
+                nc.sync.dma_start(
+                    out=dest(grp, m), in_=cos_part[:, m_cols].rearrange("p (h d) -> p h d", h=HEADS)
+                )
+
+        def rope_two(grp, m):
+            rope_products(grp, m)
+            rope_products(grp, m + 1)
+            rope_sum(nc.gpsimd, grp, [m, m + 1])
+
+        def store_plain(m):
+            ot = plain_pool.tile([P, GROUP], F32, name="plain", tag="plain")
+            b, bank = sums[("v", m)]
+            free_banks.append(b)
+            nc.scalar.copy(out=ot[:], in_=bank[:])
+            nc.sync.dma_start(out=dest("v", m), in_=ot[:].rearrange("p (h d) -> p h d", h=HEADS))
+
+        make_identity(nc, ident[:])
+        load_scale_on_k(0)
+        load_bytes(0, 0)
+        for g in range(1, PASSES):
+            load_scale_on_k(g)
+        for r in range(1, 4):
+            load_bytes(0, r)
+        for r in range(4):
+            load_rows("x", r)
+        for j, r in ((1, 0), (1, 1), (2, 0), (1, 2), (1, 3), (2, 1)):
+            load_bytes(j, r)
+        load_tables()
+        for j, r in ((2, 2), (2, 3), (3, 0), (3, 1)):
+            load_bytes(j, r)
+        for r in range(4):
+            load_rows("k", r)
+
+        for g in range(PASSES):
+            spread_scale(g)
+        scale_rows(0, 0, pieces=PASSES)
+        for r in range(1, 4):
+            scale_rows(0, r)
+        first = [(grp, a, g) for grp, a in (("x", 0), (0, 0), (0, 1), ("x", 1), (1, 0)) for g in range(PASSES)]
+        for i in range(len(first) + TURNS_AHEAD):
+            if i < len(first):
+                turn(*first[i])
+                if first[i] == (0, 0, PASSES - 1):
+                    scale_rows(1, 0)
+                    scale_rows(1, 1)
+                if first[i] == (0, 1, PASSES - 1):
+                    scale_rows(2, 0)
+            if i >= TURNS_AHEAD:
+                empty(*first[i - TURNS_AHEAD])
+        for r in range(4):
+            load_rows("v", r)
+        load_bytes(3, 2)
+        load_bytes(3, 3)
+        widen_rows(1, 2)
+        widen_rows(1, 3)
+        for grp in ("x", 0):
+            quantize(grp, 0)
+            quantize(grp, 1)
+
+
+        for m in range(TOKEN_TILES):
+            project(0, m)
+        turn(1, 1, 0)
+        turn(1, 1, 1)
+        scale_rows(2, 1)
+        widen_rows(2, 2)
+        widen_rows(2, 3)
+        rope_two(0, 0)
+        turn(1, 1, 2)
+        turn(1, 1, 3)
+        rope_two(0, 2)
+        turn_and_empty(2, 0, (0, 1))
+        for g in (0, 1):
+            empty(1, 1, g)
+            turn(2, 1, g)
+        turn_and_empty(2, 0, (2, 3))
+        for g in (2, 3):
+            empty(1, 1, g)
+            turn(2, 1, g)
+        widen_rows(3, 0)
+        widen_rows(3, 1)
+        quantize(1, 0)
+        quantize(1, 1)
+
+        for m in range(TOKEN_TILES):
+            project(1, m)
+        empty(2, 1, 0)
+        rope_two(1, 0)
+        turn_and_empty("k", 0, range(PASSES))
+        rope_two(1, 2)
+        turn_and_empty("k", 1, range(PASSES))
+        empty(2, 1, 1)
+        turn(3, 0, 0)
+        empty(2, 1, 2)
+        turn(3, 0, 1)
+        empty(2, 1, 3)
+        turn_and_empty("v", 0, (0, 1))
+        quantize(2, 0)
+        quantize(2, 1)
+        for m in range(TOKEN_TILES):
+            project(2, m)
+        quantize("k", 0)
+        quantize("k", 1)
+
+        widen_rows(3, 2)
+        widen_rows(3, 3)
+        rope_two(2, 0)
+        turn_and_empty("v", 0, (2, 3))
+        turn(3, 0, 2)
+        rope_two(2, 2)
+        turn(3, 0, 3)
+        turn_and_empty("v", 1, range(PASSES))
+        empty(3, 0, 0)
+        project("k", 0)
+        empty(3, 0, 1)
+        project("k", 1)
+        empty(3, 0, 2)
+        turn(3, 1, 0)
+        empty(3, 0, 3)
+        turn(3, 1, 1)
+        project("k", 2)
+        project("k", 3)
+        quantize("v", 0)
+        quantize("v", 1)
+
+        rope_two("k", 0)
+        turn(3, 1, 2)
+        turn(3, 1, 3)
+        for m in (0, 1):
+            project("v", m)
+            store_plain(m)
+        rope_products("k", 2)
+        rope_sum(nc.gpsimd, "k", [2])
+        for m in (2, 3):
+            project("v", m)
+            store_plain(m)
+        for g in range(PASSES):
+            empty(3, 1, g)
+        quantize(3, 0)
+        quantize(3, 1)
+
+        for m in range(TOKEN_TILES):
+            project(3, m)
+        rope_products("k", 3)
+        rope_sum(nc.gpsimd, "k", [3])
+        rope_two(3, 0)
+        rope_products(3, 2)
+        rope_products(3, 3)
+        rope_sum(nc.vector, 3, [2])
+        rope_sum(nc.vector, 3, [3])

@@ -42,8 +42,7 @@ def tile_mistralattention_kernel(
         widened_pool = ctx.enter_context(tc.tile_pool(name="widened", bufs=4))
         grouped_pool = ctx.enter_context(tc.tile_pool(name="grouped", bufs=3))
         codes_pool = ctx.enter_context(tc.tile_pool(name="codes", bufs=3))
-        cos_part_pool = ctx.enter_context(tc.tile_pool(name="cos_part", bufs=3))
-        sin_part_pool = ctx.enter_context(tc.tile_pool(name="sin_part", bufs=3))
+        parts_pool = ctx.enter_context(tc.tile_pool(name="parts", bufs=3))
         plain_pool = ctx.enter_context(tc.tile_pool(name="plain", bufs=2))
         psum = ctx.enter_context(tc.psum_pool(name="psum", bufs=1))
         ctx.enter_context(tc.manual_schedule())
@@ -51,9 +50,8 @@ def tile_mistralattention_kernel(
         ident = const.tile([P, P], F32, name="ident")
         scale_on_rows = const.tile([P, K], F32, name="scale_on_rows")
         scale_on_k = const.tile([P, PASSES, SCALE_SLOT], F32, name="scale_on_k")
-        cos_sb = const.tile([P, TOKEN_TILES, P], BF16, name="cos_sb")
-        sin_sb = const.tile([P, TOKEN_TILES, P], BF16, name="sin_sb")
-        signed_sin = const.tile([P, TOKEN_TILES, P], BF16, name="signed_sin")
+        rope_table = const.tile([P, TOKEN_TILES, 2, 2, HALF], BF16, name="rope_table")
+        low_sin = const.tile([P, TOKEN_TILES, HALF], BF16, name="low_sin")
         x_codes = const.tile([P, PASSES * GROUP], U32, name="x_codes", align_bytes=64)
         x_scales = const.tile([P, PASSES * GROUP], U8, name="x_scales", align_bytes=64)
 
@@ -94,16 +92,15 @@ def tile_mistralattention_kernel(
             )
 
         def load_tables():
-            nc.sync.dma_start(out=cos_sb[:], in_=cos.rearrange("b (t s) d -> s (b t) d", s=P))
-            nc.sync.dma_start(out=sin_sb[:], in_=sin.rearrange("b (t s) d -> s (b t) d", s=P))
+            cos_rows = cos.rearrange("b (t s) d -> s (b t) d", s=P)
+            sin_rows = sin.rearrange("b (t s) d -> s (b t) d", s=P)
+            for a in range(2):
+                nc.sync.dma_start(out=rope_table[:, :, a, 0, :], in_=cos_rows[:, :, HALF * a : HALF * (a + 1)])
+            nc.sync.dma_start(out=rope_table[:, :, 0, 1, :], in_=sin_rows[:, :, HALF:P])
+            nc.sync.dma_start(out=low_sin[:], in_=sin_rows[:, :, 0:HALF])
             nc.gpsimd.tensor_scalar(
-                out=signed_sin[:, :, 0:HALF],
-                in0=sin_sb[:, :, 0:HALF],
-                scalar1=-1.0,
-                scalar2=None,
-                op0=MULT,
+                out=rope_table[:, :, 1, 1, :], in0=low_sin[:], scalar1=-1.0, scalar2=0.0, op0=MULT, op1=ADD
             )
-            nc.gpsimd.tensor_copy(out=signed_sin[:, :, HALF:P], in_=sin_sb[:, :, HALF:P])
 
         def spread_scale(g):
             b, bank = take_bank()
@@ -219,36 +216,30 @@ def tile_mistralattention_kernel(
 
         def rope_products(grp, m):
             if m % 2 == 0:
-                ct = cos_part_pool.tile([P, 2 * GROUP], F32, name="cos_part", tag="cos_part")
-                st = sin_part_pool.tile([P, 2 * GROUP], F32, name="sin_part", tag="sin_part")
-                parts[(grp, m // 2)] = (ct, st)
-            cos_part, sin_part = parts[(grp, m // 2)]
-            cols = slice(GROUP * (m % 2), GROUP * (m % 2 + 1))
+                pt = parts_pool.tile([P, 4 * GROUP], F32, name="parts", tag="parts")
+                parts[(grp, m // 2)] = pt
+            cols = slice(2 * GROUP * (m % 2), 2 * GROUP * (m % 2 + 1))
             b, bank = sums[(grp, m)]
             free_banks.append(b)
+            shape = [P, HEADS, 2, 2, HALF]
             nc.vector.tensor_tensor(
-                out=cos_part[:, cols].rearrange("p (h d) -> p h d", h=HEADS),
-                in0=bank[:].rearrange("p (h d) -> p h d", h=HEADS),
-                in1=cos_sb[:, m : m + 1, :].to_broadcast([P, HEADS, P]),
-                op=MULT,
-            )
-            nc.vector.tensor_tensor(
-                out=sin_part[:, cols].rearrange("p (h f j) -> p h f j", h=HEADS, f=2),
-                in0=bank[:].rearrange("p (h f j) -> p h f j", h=HEADS, f=2)[:, :, ::-1, :],
-                in1=signed_sin[:, m, :]
-                .rearrange("p (o f j) -> p o f j", o=1, f=2)
-                .to_broadcast([P, HEADS, 2, HALF]),
+                out=parts[(grp, m // 2)][:, cols].rearrange("p (h a c j) -> p h a c j", h=HEADS, c=2, a=2),
+                in0=bank[:].rearrange("p (h a o j) -> p h a o j", h=HEADS, a=2, o=1).to_broadcast(shape),
+                in1=rope_table[:, m : m + 1, :, :, :].to_broadcast(shape),
                 op=MULT,
             )
 
         def rope_sum(engine, grp, ms):
-            cos_part, sin_part = parts[(grp, ms[0] // 2)]
-            cols = slice(GROUP * (ms[0] % 2), GROUP * (ms[-1] % 2 + 1))
-            engine.tensor_tensor(out=cos_part[:, cols], in0=cos_part[:, cols], in1=sin_part[:, cols], op=ADD)
+            pt = parts[(grp, ms[0] // 2)]
+            cols = slice(2 * GROUP * (ms[0] % 2), 2 * GROUP * (ms[-1] % 2 + 1))
+            blocks = pt[:, cols].rearrange("p (n q j) -> p n q j", q=4, j=HALF)
+            engine.tensor_tensor(
+                out=blocks[:, :, 0:2, :], in0=blocks[:, :, 0:4:2, :], in1=blocks[:, :, 3::-2, :], op=ADD
+            )
             for m in ms:
-                m_cols = slice(GROUP * (m % 2), GROUP * (m % 2 + 1))
+                m_cols = slice(2 * GROUP * (m % 2), 2 * GROUP * (m % 2 + 1))
                 nc.sync.dma_start(
-                    out=dest(grp, m), in_=cos_part[:, m_cols].rearrange("p (h d) -> p h d", h=HEADS)
+                    out=dest(grp, m), in_=pt[:, m_cols].rearrange("p (h c d) -> p h c d", h=HEADS, c=2)[:, :, 0, :]
                 )
 
         def rope_two(grp, m):

@@ -259,10 +259,13 @@ def tile_mistralattention_kernel(
         load_bytes(0, 0)
         for g in range(1, PASSES):
             load_scale_on_k(g)
-        for r in range(1, 4):
-            load_bytes(0, r)
-        for r in range(4):
-            load_rows("x", r)
+        load_bytes(0, 1)
+        load_rows("x", 0)
+        load_rows("x", 1)
+        load_bytes(0, 2)
+        load_rows("x", 2)
+        load_rows("x", 3)
+        load_bytes(0, 3)
         for j, r in ((1, 0), (1, 1), (2, 0), (1, 2), (1, 3), (2, 1)):
             load_bytes(j, r)
         load_tables()

@@ -243,9 +243,9 @@ def tile_mistralattention_kernel(
                 )
 
         def rope_two(grp, m):
-            rope_products(grp, m)
-            rope_products(grp, m + 1)
-            rope_sum(nc.gpsimd, grp, [m, m + 1])
+            for mm in (m, m + 1):
+                rope_products(grp, mm)
+                rope_sum(nc.gpsimd, grp, [mm])
 
         def store_plain(m):
             ot = plain_pool.tile([P, GROUP], F32, name="plain", tag="plain")
@@ -328,15 +328,15 @@ def tile_mistralattention_kernel(
         for m in range(TOKEN_TILES):
             project(1, m)
         empty(2, 1, 0)
+        empty(2, 1, 1)
         rope_two(1, 0)
         turn_and_empty("k", 0, range(PASSES))
         rope_two(1, 2)
         turn_and_empty("k", 1, range(PASSES))
-        empty(2, 1, 1)
-        turn(3, 0, 0)
         empty(2, 1, 2)
-        turn(3, 0, 1)
+        turn(3, 0, 0)
         empty(2, 1, 3)
+        turn(3, 0, 1)
         turn_and_empty("v", 0, (0, 1))
         quantize(2, 0)
         quantize(2, 1)
@@ -372,8 +372,6 @@ def tile_mistralattention_kernel(
         for m in (0, 1):
             project("v", m)
             store_plain(m)
-        rope_products("k", 2)
-        rope_sum(nc.gpsimd, "k", [2])
         for m in (2, 3):
             project("v", m)
             store_plain(m)
@@ -384,8 +382,7 @@ def tile_mistralattention_kernel(
 
         for m in range(TOKEN_TILES):
             project(3, m)
-        rope_products("k", 3)
-        rope_sum(nc.gpsimd, "k", [3])
+        rope_two("k", 2)
         rope_two(3, 0)
         rope_products(3, 2)
         rope_products(3, 3)

@@ -13,6 +13,7 @@ FP8 = mybir.dt.float8_e4m3fn
 FP8X4 = mybir.dt.float8_e4m3fn_x4
 MULT = mybir.AluOpType.mult
 ADD = mybir.AluOpType.add
+COPY = mybir.ActivationFunctionType.Copy
 
 P = 128
 K = 2048
@@ -44,6 +45,7 @@ def tile_mistralattention_kernel(
         codes_pool = ctx.enter_context(tc.tile_pool(name="codes", bufs=3))
         parts_pool = ctx.enter_context(tc.tile_pool(name="parts", bufs=3))
         plain_pool = ctx.enter_context(tc.tile_pool(name="plain", bufs=2))
+        planes_pool = ctx.enter_context(tc.tile_pool(name="planes", bufs=2))
         psum = ctx.enter_context(tc.psum_pool(name="psum", bufs=1))
         ctx.enter_context(tc.manual_schedule())
 
@@ -62,6 +64,7 @@ def tile_mistralattention_kernel(
         grouped = {}
         codes = {"x": x_codes}
         scales = {"x": x_scales}
+        planes = {}
         sums = {}
         parts = {}
 
@@ -144,16 +147,38 @@ def tile_mistralattention_kernel(
                     )
             turned[(grp, a, g)] = (b, bank)
 
-        def empty(grp, a, g):
+        def grouped_slot(grp, a, g):
             if grp not in grouped:
                 gt = grouped_pool.tile(
                     [P, PASSES * GROUP * PACK], BF16, name="grouped", tag="grouped", align_bytes=64
                 )
                 grouped[grp] = gt
+            c0 = GROUP * PACK * g + 2 * P * PACK * a
+            return grouped[grp][:, c0 : c0 + 2 * P * PACK]
+
+        def scale_out(j, a, g):
+            b, bank = turned[(j, a, g)]
+            free_banks.append(b)
+            pl = planes_pool.tile([P, PACK, 2 * P], BF16, name="planes", tag="planes")
+            planes[(j, a, g)] = pl
+            values = bank[:].bitcast(BF16).rearrange("p (u r e) -> p u r e", u=2, e=2)
+            for t in range(PACK):
+                nc.scalar.activation(
+                    out=pl[:, t, :], in_=values[:, t // 2, :, t % 2], func=COPY, scale=scale_on_k[:, g, t : t + 1]
+                )
+
+        def interleave(engine_name, j, a, g):
+            dst = grouped_slot(j, a, g).rearrange("p (r t) -> p r t", t=PACK)
+            src = planes[(j, a, g)][:].rearrange("p t r -> p r t")
+            if engine_name == "gpsimd":
+                nc.gpsimd.tensor_scalar(out=dst, in0=src, scalar1=1.0, scalar2=0.0, op0=MULT, op1=ADD)
+            else:
+                nc.scalar.copy(out=dst, in_=src)
+
+        def empty(grp, a, g):
             b, bank = turned[(grp, a, g)]
             free_banks.append(b)
-            c0 = GROUP * PACK * g + 2 * P * PACK * a
-            dst = grouped[grp][:, c0 : c0 + 2 * P * PACK]
+            dst = grouped_slot(grp, a, g)
             if needs_scale[(grp, 2 * a)]:
                 nc.vector.tensor_tensor(
                     out=dst.rearrange("p (r u e) -> p r u e", u=2, e=2),
@@ -303,23 +328,25 @@ def tile_mistralattention_kernel(
 
         for m in range(TOKEN_TILES):
             project(0, m)
+        turn(1, 1, 3)
         turn(1, 1, 0)
-        turn(1, 1, 1)
         scale_rows(2, 1)
         widen_rows(2, 2)
+        scale_out(1, 1, 3)
         widen_rows(2, 3)
         rope_two(0, 0)
+        turn(1, 1, 1)
         turn(1, 1, 2)
-        turn(1, 1, 3)
         rope_two(0, 2)
+        interleave("gpsimd", 1, 1, 3)
         turn_and_empty(2, 0, (0, 1))
         for g in (0, 1):
             empty(1, 1, g)
             turn(2, 1, g)
         turn_and_empty(2, 0, (2, 3))
-        for g in (2, 3):
-            empty(1, 1, g)
-            turn(2, 1, g)
+        empty(1, 1, 2)
+        turn(2, 1, 2)
+        turn(2, 1, 3)
         widen_rows(3, 0)
         widen_rows(3, 1)
         quantize(1, 0)
@@ -348,34 +375,37 @@ def tile_mistralattention_kernel(
         widen_rows(3, 2)
         widen_rows(3, 3)
         rope_two(2, 0)
+        turn(3, 0, 3)
+        scale_out(3, 0, 3)
         turn_and_empty("v", 0, (2, 3))
         turn(3, 0, 2)
         rope_two(2, 2)
-        turn(3, 0, 3)
+        interleave("gpsimd", 3, 0, 3)
         turn_and_empty("v", 1, range(PASSES))
         empty(3, 0, 0)
         project("k", 0)
         empty(3, 0, 1)
         project("k", 1)
         empty(3, 0, 2)
+        turn(3, 1, 3)
+        scale_out(3, 1, 3)
         turn(3, 1, 0)
-        empty(3, 0, 3)
-        turn(3, 1, 1)
         project("k", 2)
         project("k", 3)
         quantize("v", 0)
         quantize("v", 1)
 
         rope_two("k", 0)
+        interleave("gpsimd", 3, 1, 3)
+        turn(3, 1, 1)
         turn(3, 1, 2)
-        turn(3, 1, 3)
         for m in (0, 1):
             project("v", m)
             store_plain(m)
         for m in (2, 3):
             project("v", m)
             store_plain(m)
-        for g in range(PASSES):
+        for g in range(3):
             empty(3, 1, g)
         quantize(3, 0)
         quantize(3, 1)

@@ -212,9 +212,11 @@ def tile_mistralattention_kernel(
                 in_=grouped[grp][:, 2 * GROUP * PACK * h : 2 * GROUP * PACK * (h + 1)],
             )
 
-        def project(grp, m):
-            b, bank = take_bank()
-            for g in range(PASSES):
+        def project(grp, m, passes=(0, 1, 2, 3)):
+            if passes[0] == 0:
+                sums[(grp, m)] = take_bank()
+            b, bank = sums[(grp, m)]
+            for g in passes:
                 x_cols = slice(GROUP * g + P * m, GROUP * g + P * (m + 1))
                 w_cols = slice(GROUP * g, GROUP * (g + 1))
                 nc.tensor.matmul_mx(
@@ -226,7 +228,16 @@ def tile_mistralattention_kernel(
                     start=(g == 0),
                     stop=(g == PASSES - 1),
                 )
-            sums[(grp, m)] = (b, bank)
+
+        def quantize_and_project(grp):
+            quantize(grp, 0)
+            project(grp, 0, (0, 1))
+            project(grp, 1, (0, 1))
+            quantize(grp, 1)
+            project(grp, 0, (2, 3))
+            project(grp, 1, (2, 3))
+            project(grp, 2)
+            project(grp, 3)
 
         def dest(grp, m):
             batch = m // 2
@@ -321,13 +332,11 @@ def tile_mistralattention_kernel(
         load_bytes(3, 3)
         widen_rows(1, 2)
         widen_rows(1, 3)
-        for grp in ("x", 0):
-            quantize(grp, 0)
-            quantize(grp, 1)
+        quantize("x", 0)
+        quantize("x", 1)
+        quantize_and_project(0)
 
 
-        for m in range(TOKEN_TILES):
-            project(0, m)
         turn(1, 1, 3)
         turn(1, 1, 0)
         scale_rows(2, 1)
@@ -338,7 +347,7 @@ def tile_mistralattention_kernel(
         turn(1, 1, 1)
         turn(1, 1, 2)
         rope_two(0, 2)
-        interleave("gpsimd", 1, 1, 3)
+        interleave("scalar", 1, 1, 3)
         turn_and_empty(2, 0, (0, 1))
         for g in (0, 1):
             empty(1, 1, g)
@@ -349,11 +358,8 @@ def tile_mistralattention_kernel(
         turn(2, 1, 3)
         widen_rows(3, 0)
         widen_rows(3, 1)
-        quantize(1, 0)
-        quantize(1, 1)
+        quantize_and_project(1)
 
-        for m in range(TOKEN_TILES):
-            project(1, m)
         empty(2, 1, 0)
         empty(2, 1, 1)
         rope_two(1, 0)
@@ -365,23 +371,20 @@ def tile_mistralattention_kernel(
         empty(2, 1, 3)
         turn(3, 0, 1)
         turn_and_empty("v", 0, (0, 1))
-        quantize(2, 0)
-        quantize(2, 1)
-        for m in range(TOKEN_TILES):
-            project(2, m)
+        quantize_and_project(2)
         quantize("k", 0)
         quantize("k", 1)
 
         widen_rows(3, 2)
         widen_rows(3, 3)
         rope_two(2, 0)
-        turn(3, 0, 3)
-        scale_out(3, 0, 3)
         turn_and_empty("v", 0, (2, 3))
         turn(3, 0, 2)
         rope_two(2, 2)
-        interleave("gpsimd", 3, 0, 3)
         turn_and_empty("v", 1, range(PASSES))
+        turn(3, 0, 3)
+        scale_out(3, 0, 3)
+        interleave("scalar", 3, 0, 3)
         empty(3, 0, 0)
         project("k", 0)
         empty(3, 0, 1)
@@ -390,14 +393,14 @@ def tile_mistralattention_kernel(
         turn(3, 1, 3)
         scale_out(3, 1, 3)
         turn(3, 1, 0)
+        turn(3, 1, 1)
         project("k", 2)
         project("k", 3)
         quantize("v", 0)
         quantize("v", 1)
 
         rope_two("k", 0)
-        interleave("gpsimd", 3, 1, 3)
-        turn(3, 1, 1)
+        interleave("scalar", 3, 1, 3)
         turn(3, 1, 2)
         for m in (0, 1):
             project("v", m)
@@ -407,11 +410,8 @@ def tile_mistralattention_kernel(
             store_plain(m)
         for g in range(3):
             empty(3, 1, g)
-        quantize(3, 0)
-        quantize(3, 1)
+        quantize_and_project(3)
 
-        for m in range(TOKEN_TILES):
-            project(3, m)
         rope_two("k", 2)
         rope_two(3, 0)
         rope_products(3, 2)

@@ -402,13 +402,15 @@ def tile_mistralattention_kernel(
         rope_two("k", 0)
         interleave("scalar", 3, 1, 3)
         turn(3, 1, 2)
+        scale_out(3, 1, 2)
+        interleave("scalar", 3, 1, 2)
         for m in (0, 1):
             project("v", m)
             store_plain(m)
         for m in (2, 3):
             project("v", m)
             store_plain(m)
-        for g in range(3):
+        for g in range(2):
             empty(3, 1, g)
         quantize_and_project(3)
 

@@ -392,6 +392,8 @@ def tile_mistralattention_kernel(
         empty(3, 0, 2)
         turn(3, 1, 3)
         scale_out(3, 1, 3)
+        turn(3, 1, 2)
+        scale_out(3, 1, 2)
         turn(3, 1, 0)
         turn(3, 1, 1)
         project("k", 2)
@@ -401,8 +403,6 @@ def tile_mistralattention_kernel(
 
         rope_two("k", 0)
         interleave("scalar", 3, 1, 3)
-        turn(3, 1, 2)
-        scale_out(3, 1, 2)
         interleave("scalar", 3, 1, 2)
         for m in (0, 1):
             project("v", m)

@@ -232,10 +232,9 @@ def tile_mistralattention_kernel(
         def quantize_and_project(grp):
             quantize(grp, 0)
             project(grp, 0, (0, 1))
-            project(grp, 1, (0, 1))
             quantize(grp, 1)
             project(grp, 0, (2, 3))
-            project(grp, 1, (2, 3))
+            project(grp, 1)
             project(grp, 2)
             project(grp, 3)
 
@@ -332,6 +331,7 @@ def tile_mistralattention_kernel(
         load_bytes(3, 3)
         widen_rows(1, 2)
         widen_rows(1, 3)
+        widen_rows(2, 3)
         quantize("x", 0)
         quantize("x", 1)
         quantize_and_project(0)
@@ -342,7 +342,6 @@ def tile_mistralattention_kernel(
         scale_rows(2, 1)
         widen_rows(2, 2)
         scale_out(1, 1, 3)
-        widen_rows(2, 3)
         rope_two(0, 0)
         turn(1, 1, 1)
         turn(1, 1, 2)
@@ -366,36 +365,44 @@ def tile_mistralattention_kernel(
         turn_and_empty("k", 0, range(PASSES))
         rope_two(1, 2)
         turn_and_empty("k", 1, range(PASSES))
+        widen_rows(3, 2)
         empty(2, 1, 2)
         turn(3, 0, 0)
+        turn("v", 0, 2)
         empty(2, 1, 3)
         turn(3, 0, 1)
+        turn("v", 0, 3)
         turn_and_empty("v", 0, (0, 1))
         quantize_and_project(2)
         quantize("k", 0)
         quantize("k", 1)
 
-        widen_rows(3, 2)
-        widen_rows(3, 3)
         rope_two(2, 0)
-        turn_and_empty("v", 0, (2, 3))
-        turn(3, 0, 2)
+        widen_rows(3, 3)
+        empty("v", 0, 2)
+        empty("v", 0, 3)
         rope_two(2, 2)
-        turn_and_empty("v", 1, range(PASSES))
-        turn(3, 0, 3)
-        scale_out(3, 0, 3)
-        interleave("scalar", 3, 0, 3)
+        turn_and_empty("v", 1, (0, 1))
+        turn(3, 0, 2)
         empty(3, 0, 0)
-        project("k", 0)
-        empty(3, 0, 1)
-        project("k", 1)
-        empty(3, 0, 2)
-        turn(3, 1, 3)
-        scale_out(3, 1, 3)
         turn(3, 1, 2)
-        scale_out(3, 1, 2)
+        scale_out(3, 0, 2)
+        turn("v", 1, 2)
+        turn(3, 1, 3)
+        empty("v", 1, 2)
+        turn("v", 1, 3)
+        interleave("scalar", 3, 0, 2)
+        turn(3, 0, 3)
+        empty("v", 1, 3)
         turn(3, 1, 0)
+        scale_out(3, 0, 3)
         turn(3, 1, 1)
+        interleave("scalar", 3, 0, 3)
+        empty(3, 0, 1)
+        project("k", 0)
+        project("k", 1)
+        scale_out(3, 1, 3)
+        scale_out(3, 1, 2)
         project("k", 2)
         project("k", 3)
         quantize("v", 0)
@@ -404,14 +411,16 @@ def tile_mistralattention_kernel(
         rope_two("k", 0)
         interleave("scalar", 3, 1, 3)
         interleave("scalar", 3, 1, 2)
-        for m in (0, 1):
-            project("v", m)
-            store_plain(m)
-        for m in (2, 3):
-            project("v", m)
-            store_plain(m)
-        for g in range(2):
-            empty(3, 1, g)
+        project("v", 0)
+        empty(3, 1, 0)
+        store_plain(0)
+        project("v", 1)
+        store_plain(1)
+        project("v", 2)
+        empty(3, 1, 1)
+        store_plain(2)
+        project("v", 3)
+        store_plain(3)
         quantize_and_project(3)
 
         rope_two("k", 2)

@@ -232,9 +232,10 @@ def tile_mistralattention_kernel(
         def quantize_and_project(grp):
             quantize(grp, 0)
             project(grp, 0, (0, 1))
+            project(grp, 1, (0, 1))
             quantize(grp, 1)
             project(grp, 0, (2, 3))
-            project(grp, 1)
+            project(grp, 1, (2, 3))
             project(grp, 2)
             project(grp, 3)
 
@@ -301,52 +302,65 @@ def tile_mistralattention_kernel(
         load_rows("x", 2)
         load_rows("x", 3)
         load_bytes(0, 3)
-        for j, r in ((1, 0), (1, 1), (2, 0), (1, 2), (1, 3), (2, 1)):
+        load_rows("v", 0)
+        load_rows("v", 1)
+        load_bytes(1, 0)
+        load_bytes(1, 1)
+        load_rows("v", 2)
+        load_rows("v", 3)
+        for j, r in ((2, 0), (1, 2), (1, 3), (2, 1)):
             load_bytes(j, r)
         load_tables()
         for j, r in ((2, 2), (2, 3), (3, 0), (3, 1)):
             load_bytes(j, r)
-        for r in range(4):
-            load_rows("k", r)
 
         for g in range(PASSES):
             spread_scale(g)
         scale_rows(0, 0, pieces=PASSES)
         for r in range(1, 4):
             scale_rows(0, r)
-        first = [(grp, a, g) for grp, a in (("x", 0), (0, 0), (0, 1), ("x", 1), (1, 0)) for g in range(PASSES)]
+        first = [(grp, a, g) for grp, a in (("x", 0), (0, 0), ("x", 1), ("v", 0), (0, 1), ("v", 1), (1, 0)) for g in range(PASSES)]
         for i in range(len(first) + TURNS_AHEAD):
             if i < len(first):
                 turn(*first[i])
                 if first[i] == (0, 0, PASSES - 1):
                     scale_rows(1, 0)
                     scale_rows(1, 1)
-                if first[i] == (0, 1, PASSES - 1):
-                    scale_rows(2, 0)
             if i >= TURNS_AHEAD:
                 empty(*first[i - TURNS_AHEAD])
+                if first[i - TURNS_AHEAD] == ("x", 1, PASSES - 1):
+                    quantize("x", 0)
+                    quantize("x", 1)
+                if first[i - TURNS_AHEAD] == ("v", 1, PASSES - 1):
+                    quantize("v", 0)
+                    quantize("v", 1)
         for r in range(4):
-            load_rows("v", r)
+            load_rows("k", r)
         load_bytes(3, 2)
         load_bytes(3, 3)
         widen_rows(1, 2)
+        for m in (0, 1):
+            project("v", m)
+            store_plain(m)
         widen_rows(1, 3)
-        widen_rows(2, 3)
-        quantize("x", 0)
-        quantize("x", 1)
         quantize_and_project(0)
-
+        scale_rows(2, 0)
+        scale_rows(2, 1)
+        widen_rows(2, 3)
+        widen_rows(2, 2)
 
         turn(1, 1, 3)
         turn(1, 1, 0)
-        scale_rows(2, 1)
-        widen_rows(2, 2)
-        scale_out(1, 1, 3)
-        rope_two(0, 0)
         turn(1, 1, 1)
         turn(1, 1, 2)
+        rope_two(0, 0)
+        project("v", 2)
+        project("v", 3)
         rope_two(0, 2)
+        scale_out(1, 1, 3)
         interleave("scalar", 1, 1, 3)
+        store_plain(2)
+        store_plain(3)
         turn_and_empty(2, 0, (0, 1))
         for g in (0, 1):
             empty(1, 1, g)
@@ -368,59 +382,39 @@ def tile_mistralattention_kernel(
         widen_rows(3, 2)
         empty(2, 1, 2)
         turn(3, 0, 0)
-        turn("v", 0, 2)
         empty(2, 1, 3)
+        turn(3, 0, 2)
         turn(3, 0, 1)
-        turn("v", 0, 3)
-        turn_and_empty("v", 0, (0, 1))
+        widen_rows(3, 3)
         quantize_and_project(2)
         quantize("k", 0)
         quantize("k", 1)
 
         rope_two(2, 0)
-        widen_rows(3, 3)
-        empty("v", 0, 2)
-        empty("v", 0, 3)
-        rope_two(2, 2)
-        turn_and_empty("v", 1, (0, 1))
-        turn(3, 0, 2)
-        empty(3, 0, 0)
-        turn(3, 1, 2)
         scale_out(3, 0, 2)
-        turn("v", 1, 2)
-        turn(3, 1, 3)
-        empty("v", 1, 2)
-        turn("v", 1, 3)
-        interleave("scalar", 3, 0, 2)
         turn(3, 0, 3)
-        empty("v", 1, 3)
-        turn(3, 1, 0)
         scale_out(3, 0, 3)
-        turn(3, 1, 1)
-        interleave("scalar", 3, 0, 3)
-        empty(3, 0, 1)
+        rope_two(2, 2)
+        turn(3, 1, 2)
+        interleave("scalar", 3, 0, 2)
         project("k", 0)
-        project("k", 1)
-        scale_out(3, 1, 3)
+        turn(3, 1, 3)
+        interleave("scalar", 3, 0, 3)
+        empty(3, 0, 0)
+        turn(3, 1, 0)
         scale_out(3, 1, 2)
+        empty(3, 0, 1)
+        turn(3, 1, 1)
+        scale_out(3, 1, 3)
+        project("k", 1)
+        interleave("scalar", 3, 1, 2)
+        interleave("scalar", 3, 1, 3)
         project("k", 2)
         project("k", 3)
-        quantize("v", 0)
-        quantize("v", 1)
 
         rope_two("k", 0)
-        interleave("scalar", 3, 1, 3)
-        interleave("scalar", 3, 1, 2)
-        project("v", 0)
         empty(3, 1, 0)
-        store_plain(0)
-        project("v", 1)
-        store_plain(1)
-        project("v", 2)
         empty(3, 1, 1)
-        store_plain(2)
-        project("v", 3)
-        store_plain(3)
         quantize_and_project(3)
 
         rope_two("k", 2)

@@ -101,9 +101,9 @@ def tile_mistralattention_kernel(
                 nc.sync.dma_start(out=rope_table[:, :, a, 0, :], in_=cos_rows[:, :, HALF * a : HALF * (a + 1)])
             nc.sync.dma_start(out=rope_table[:, :, 0, 1, :], in_=sin_rows[:, :, HALF:P])
             nc.sync.dma_start(out=low_sin[:], in_=sin_rows[:, :, 0:HALF])
-            nc.gpsimd.tensor_scalar(
-                out=rope_table[:, :, 1, 1, :], in0=low_sin[:], scalar1=-1.0, scalar2=0.0, op0=MULT, op1=ADD
-            )
+
+        def negate_low_sin():
+            nc.scalar.activation(out=rope_table[:, :, 1, 1, :], in_=low_sin[:], func=COPY, scale=-1.0)
 
         def spread_scale(g):
             b, bank = take_bank()
@@ -302,9 +302,9 @@ def tile_mistralattention_kernel(
         load_rows("x", 2)
         load_rows("x", 3)
         load_bytes(0, 3)
+        load_bytes(1, 0)
         load_rows("v", 0)
         load_rows("v", 1)
-        load_bytes(1, 0)
         load_bytes(1, 1)
         load_rows("v", 2)
         load_rows("v", 3)
@@ -331,6 +331,8 @@ def tile_mistralattention_kernel(
                 if first[i - TURNS_AHEAD] == ("x", 1, PASSES - 1):
                     quantize("x", 0)
                     quantize("x", 1)
+                if first[i - TURNS_AHEAD] == (0, 1, PASSES - 1):
+                    quantize(0, 0)
                 if first[i - TURNS_AHEAD] == ("v", 1, PASSES - 1):
                     quantize("v", 0)
                     quantize("v", 1)
@@ -338,37 +340,47 @@ def tile_mistralattention_kernel(
             load_rows("k", r)
         load_bytes(3, 2)
         load_bytes(3, 3)
+        negate_low_sin()
         widen_rows(1, 2)
         for m in (0, 1):
             project("v", m)
             store_plain(m)
         widen_rows(1, 3)
-        quantize_and_project(0)
+        project(0, 0, (0, 1))
+        project(0, 1, (0, 1))
+        quantize(0, 1)
+        project(0, 0, (2, 3))
+        project(0, 1, (2, 3))
+        project(0, 2)
+        project(0, 3)
         scale_rows(2, 0)
         scale_rows(2, 1)
         widen_rows(2, 3)
         widen_rows(2, 2)
 
-        turn(1, 1, 3)
-        turn(1, 1, 0)
-        turn(1, 1, 1)
-        turn(1, 1, 2)
+        for g in range(PASSES):
+            turn(1, 1, g)
         rope_two(0, 0)
         project("v", 2)
         project("v", 3)
-        rope_two(0, 2)
+        rope_products(0, 2)
+        rope_sum(nc.gpsimd, 0, [2])
+        empty(1, 1, 0)
+        rope_products(0, 3)
+        rope_sum(nc.gpsimd, 0, [3])
+        empty(1, 1, 1)
         scale_out(1, 1, 3)
         interleave("scalar", 1, 1, 3)
-        store_plain(2)
         store_plain(3)
-        turn_and_empty(2, 0, (0, 1))
-        for g in (0, 1):
-            empty(1, 1, g)
-            turn(2, 1, g)
-        turn_and_empty(2, 0, (2, 3))
+        turn(2, 0, 0)
         empty(1, 1, 2)
-        turn(2, 1, 2)
-        turn(2, 1, 3)
+        empty(2, 0, 0)
+        turn(2, 0, 1)
+        turn(2, 1, 0)
+        turn(2, 1, 1)
+        store_plain(2)
+        turn_and_empty(2, 0, (2, 3))
+        empty(2, 0, 1)
         widen_rows(3, 0)
         widen_rows(3, 1)
         quantize_and_project(1)
@@ -376,8 +388,16 @@ def tile_mistralattention_kernel(
         empty(2, 1, 0)
         empty(2, 1, 1)
         rope_two(1, 0)
-        turn_and_empty("k", 0, range(PASSES))
-        rope_two(1, 2)
+        turn_and_empty("k", 0, (0,))
+        turn("k", 0, 1)
+        turn(2, 1, 2)
+        empty("k", 0, 1)
+        turn_and_empty("k", 0, (2, 3))
+        rope_products(1, 2)
+        rope_sum(nc.gpsimd, 1, [2])
+        turn(2, 1, 3)
+        rope_products(1, 3)
+        rope_sum(nc.gpsimd, 1, [3])
         turn_and_empty("k", 1, range(PASSES))
         widen_rows(3, 2)
         empty(2, 1, 2)

@@ -403,8 +403,10 @@ def tile_mistralattention_kernel(
         empty(2, 1, 2)
         turn(3, 0, 0)
         empty(2, 1, 3)
-        turn(3, 0, 2)
         turn(3, 0, 1)
+        scale_out(3, 0, 1)
+        interleave("scalar", 3, 0, 1)
+        turn(3, 0, 2)
         widen_rows(3, 3)
         quantize_and_project(2)
         quantize("k", 0)
@@ -423,7 +425,6 @@ def tile_mistralattention_kernel(
         empty(3, 0, 0)
         turn(3, 1, 0)
         scale_out(3, 1, 2)
-        empty(3, 0, 1)
         turn(3, 1, 1)
         scale_out(3, 1, 3)
         project("k", 1)

@@ -54,8 +54,8 @@ def tile_mistralattention_kernel(
         scale_on_k = const.tile([P, PASSES, SCALE_SLOT], F32, name="scale_on_k")
         rope_table = const.tile([P, TOKEN_TILES, 2, 2, HALF], BF16, name="rope_table")
         low_sin = const.tile([P, TOKEN_TILES, HALF], BF16, name="low_sin")
-        x_codes = const.tile([P, PASSES * GROUP], U32, name="x_codes", align_bytes=64)
-        x_scales = const.tile([P, PASSES * GROUP], U8, name="x_scales", align_bytes=64)
+        x_codes = const.tile([P, PASSES * GROUP], U32, name="x_codes", align_bytes=256)
+        x_scales = const.tile([P, PASSES * GROUP], U8, name="x_scales", align_bytes=256)
 
         q_bytes = {}
         row_tiles = {}
@@ -150,7 +150,7 @@ def tile_mistralattention_kernel(
         def grouped_slot(grp, a, g):
             if grp not in grouped:
                 gt = grouped_pool.tile(
-                    [P, PASSES * GROUP * PACK], BF16, name="grouped", tag="grouped", align_bytes=64
+                    [P, PASSES * GROUP * PACK], BF16, name="grouped", tag="grouped", align_bytes=256
                 )
                 grouped[grp] = gt
             c0 = GROUP * PACK * g + 2 * P * PACK * a
@@ -201,8 +201,8 @@ def tile_mistralattention_kernel(
 
         def quantize(grp, h):
             if h == 0 and grp != "x":
-                ct = codes_pool.tile([P, PASSES * GROUP], U32, name="codes", tag="codes", align_bytes=64)
-                st = codes_pool.tile([P, PASSES * GROUP], U8, name="scales", tag="scales", align_bytes=64)
+                ct = codes_pool.tile([P, PASSES * GROUP], U32, name="codes", tag="codes", align_bytes=256)
+                st = codes_pool.tile([P, PASSES * GROUP], U8, name="scales", tag="scales", align_bytes=256)
                 codes[grp] = ct
                 scales[grp] = st
             cols = slice(2 * GROUP * h, 2 * GROUP * (h + 1))

@@ -342,51 +342,55 @@ def tile_mistralattention_kernel(
         load_bytes(3, 3)
         negate_low_sin()
         widen_rows(1, 2)
-        for m in (0, 1):
-            project("v", m)
-            store_plain(m)
         widen_rows(1, 3)
         project(0, 0, (0, 1))
         project(0, 1, (0, 1))
+        for m in (0, 1):
+            project("v", m)
+            store_plain(m)
         quantize(0, 1)
         project(0, 0, (2, 3))
         project(0, 1, (2, 3))
         project(0, 2)
+        turn(1, 1, 2)
+        turn(1, 1, 3)
         project(0, 3)
+        turn(1, 1, 0)
+        turn(1, 1, 1)
         scale_rows(2, 0)
         scale_rows(2, 1)
         widen_rows(2, 3)
         widen_rows(2, 2)
+        scale_out(1, 1, 2)
+        scale_out(1, 1, 3)
+        interleave("scalar", 1, 1, 2)
+        interleave("scalar", 1, 1, 3)
 
-        for g in range(PASSES):
-            turn(1, 1, g)
         rope_two(0, 0)
         project("v", 2)
         project("v", 3)
-        rope_products(0, 2)
-        rope_sum(nc.gpsimd, 0, [2])
+        rope_two(0, 2)
         empty(1, 1, 0)
-        rope_products(0, 3)
-        rope_sum(nc.gpsimd, 0, [3])
         empty(1, 1, 1)
-        scale_out(1, 1, 3)
-        interleave("scalar", 1, 1, 3)
+        store_plain(2)
         store_plain(3)
         turn(2, 0, 0)
-        empty(1, 1, 2)
-        empty(2, 0, 0)
         turn(2, 0, 1)
-        turn(2, 1, 0)
-        turn(2, 1, 1)
-        store_plain(2)
-        turn_and_empty(2, 0, (2, 3))
+        empty(2, 0, 0)
         empty(2, 0, 1)
+        turn(2, 1, 1)
+        turn(2, 0, 2)
+        turn(2, 0, 3)
+        scale_out(2, 1, 1)
+        empty(2, 0, 2)
+        empty(2, 0, 3)
+        interleave("scalar", 2, 1, 1)
+        turn(2, 1, 0)
         widen_rows(3, 0)
         widen_rows(3, 1)
         quantize_and_project(1)
 
         empty(2, 1, 0)
-        empty(2, 1, 1)
         rope_two(1, 0)
         turn_and_empty("k", 0, (0,))
         turn("k", 0, 1)
@@ -409,6 +413,7 @@ def tile_mistralattention_kernel(
         turn(3, 0, 2)
         widen_rows(3, 3)
         quantize_and_project(2)
+        empty(3, 0, 0)
         quantize("k", 0)
         quantize("k", 1)
 
@@ -422,7 +427,6 @@ def tile_mistralattention_kernel(
         project("k", 0)
         turn(3, 1, 3)
         interleave("scalar", 3, 0, 3)
-        empty(3, 0, 0)
         turn(3, 1, 0)
         scale_out(3, 1, 2)
         turn(3, 1, 1)
@@ -433,12 +437,25 @@ def tile_mistralattention_kernel(
         project("k", 2)
         project("k", 3)
 
-        rope_two("k", 0)
+        rope_products("k", 0)
+        rope_sum(nc.gpsimd, "k", [0])
         empty(3, 1, 0)
         empty(3, 1, 1)
-        quantize_and_project(3)
+        rope_products("k", 1)
+        rope_sum(nc.gpsimd, "k", [1])
+        quantize(3, 0)
+        project(3, 0, (0, 1))
+        project(3, 1, (0, 1))
+        rope_products("k", 2)
+        rope_sum(nc.gpsimd, "k", [2])
+        quantize(3, 1)
+        project(3, 0, (2, 3))
+        project(3, 1, (2, 3))
+        project(3, 2)
+        project(3, 3)
 
-        rope_two("k", 2)
+        rope_products("k", 3)
+        rope_sum(nc.gpsimd, "k", [3])
         rope_two(3, 0)
         rope_products(3, 2)
         rope_products(3, 3)

@@ -168,8 +168,8 @@ def tile_mistralattention_kernel(
                 )
 
         def interleave(engine_name, j, a, g):
-            dst = grouped_slot(j, a, g).rearrange("p (r t) -> p r t", t=PACK)
-            src = planes[(j, a, g)][:].rearrange("p t r -> p r t")
+            dst = grouped_slot(j, a, g).rearrange("p (c i t) -> p c t i", i=4, t=PACK)
+            src = planes[(j, a, g)][:].rearrange("p t (c i) -> p c t i", i=4)
             if engine_name == "gpsimd":
                 nc.gpsimd.tensor_scalar(out=dst, in0=src, scalar1=1.0, scalar2=0.0, op0=MULT, op1=ADD)
             else:

@@ -56,14 +56,16 @@ def tile_mistralattention_kernel(
         low_sin = const.tile([P, TOKEN_TILES, HALF], BF16, name="low_sin")
         x_codes = const.tile([P, PASSES * GROUP], U32, name="x_codes", align_bytes=256)
         x_scales = const.tile([P, PASSES * GROUP], U8, name="x_scales", align_bytes=256)
+        v_codes = const.tile([P, PASSES * GROUP], U32, name="v_codes", align_bytes=256)
+        v_scales = const.tile([P, PASSES * GROUP], U8, name="v_scales", align_bytes=256)
 
         q_bytes = {}
         row_tiles = {}
         needs_scale = {}
         turned = {}
         grouped = {}
-        codes = {"x": x_codes}
-        scales = {"x": x_scales}
+        codes = {"x": x_codes, "v": v_codes}
+        scales = {"x": x_scales, "v": v_scales}
         planes = {}
         sums = {}
         parts = {}
@@ -200,7 +202,7 @@ def tile_mistralattention_kernel(
                 empty(grp, a, g)
 
         def quantize(grp, h):
-            if h == 0 and grp != "x":
+            if h == 0 and grp not in ("x", "v"):
                 ct = codes_pool.tile([P, PASSES * GROUP], U32, name="codes", tag="codes", align_bytes=256)
                 st = codes_pool.tile([P, PASSES * GROUP], U8, name="scales", tag="scales", align_bytes=256)
                 codes[grp] = ct
@@ -367,13 +369,9 @@ def tile_mistralattention_kernel(
         interleave("scalar", 1, 1, 3)
 
         rope_two(0, 0)
-        project("v", 2)
-        project("v", 3)
         rope_two(0, 2)
         empty(1, 1, 0)
         empty(1, 1, 1)
-        store_plain(2)
-        store_plain(3)
         turn(2, 0, 0)
         turn(2, 0, 1)
         empty(2, 0, 0)
@@ -443,6 +441,10 @@ def tile_mistralattention_kernel(
         empty(3, 1, 1)
         rope_products("k", 1)
         rope_sum(nc.gpsimd, "k", [1])
+        project("v", 2)
+        project("v", 3)
+        store_plain(2)
+        store_plain(3)
         quantize(3, 0)
         project(3, 0, (0, 1))
         project(3, 1, (0, 1))

@@ -384,17 +384,14 @@ def tile_mistralattention_kernel(
         empty(2, 0, 3)
         interleave("scalar", 2, 1, 1)
         turn(2, 1, 0)
+        turn_and_empty("k", 0, range(PASSES))
         widen_rows(3, 0)
         widen_rows(3, 1)
         quantize_and_project(1)
 
         empty(2, 1, 0)
         rope_two(1, 0)
-        turn_and_empty("k", 0, (0,))
-        turn("k", 0, 1)
         turn(2, 1, 2)
-        empty("k", 0, 1)
-        turn_and_empty("k", 0, (2, 3))
         rope_products(1, 2)
         rope_sum(nc.gpsimd, 1, [2])
         turn(2, 1, 3)

from contextlib import ExitStack

import concourse.mybir as mybir
from concourse.masks import make_identity

FLOPS = 2 * 512 * 2048 * 3072

F32 = mybir.dt.float32
BF16 = mybir.dt.bfloat16
U8 = mybir.dt.uint8
U32 = mybir.dt.uint32
FP8 = mybir.dt.float8_e4m3fn
FP8X4 = mybir.dt.float8_e4m3fn_x4
MULT = mybir.AluOpType.mult
ADD = mybir.AluOpType.add
COPY = mybir.ActivationFunctionType.Copy

P = 128
K = 2048
PASSES = 4
PASS_K = K // PASSES
PACK = 4
GROUP = 512
HEADS = GROUP // P
HALF = P // 2
TOKEN_TILES = 4
PSUM_BANKS = 8
SCALE_SLOT = 8
TURNS_AHEAD = 3


def tile_mistralattention_kernel(
    tc, hidden_states, cos, sin, q_w_bytes, q_w_scale, k_w, v_w, out_0, out_1, out_2
):
    nc = tc.nc
    rows_of = {"x": hidden_states.flatten_outer_dims(), "k": k_w, "v": v_w}

    with ExitStack() as ctx:
        const = ctx.enter_context(tc.tile_pool(name="const", bufs=1))
        bytes_pool = ctx.enter_context(tc.tile_pool(name="bytes", bufs=16))
        rows_pool = ctx.enter_context(tc.tile_pool(name="rows", bufs=8))
        scaled_pool = ctx.enter_context(tc.tile_pool(name="scaled", bufs=4))
        widened_pool = ctx.enter_context(tc.tile_pool(name="widened", bufs=4))
        grouped_pool = ctx.enter_context(tc.tile_pool(name="grouped", bufs=3))
        codes_pool = ctx.enter_context(tc.tile_pool(name="codes", bufs=3))
        parts_pool = ctx.enter_context(tc.tile_pool(name="parts", bufs=3))
        plain_pool = ctx.enter_context(tc.tile_pool(name="plain", bufs=2))
        planes_pool = ctx.enter_context(tc.tile_pool(name="planes", bufs=2))
        psum = ctx.enter_context(tc.psum_pool(name="psum", bufs=1))
        ctx.enter_context(tc.manual_schedule())

        ident = const.tile([P, P], F32, name="ident")
        scale_on_rows = const.tile([P, K], F32, name="scale_on_rows")
        scale_on_k = const.tile([P, PASSES, SCALE_SLOT], F32, name="scale_on_k")
        rope_table = const.tile([P, TOKEN_TILES, 2, 2, HALF], BF16, name="rope_table")
        low_sin = const.tile([P, TOKEN_TILES, HALF], BF16, name="low_sin")
        x_codes = const.tile([P, PASSES * GROUP], U32, name="x_codes", align_bytes=256)
        x_scales = const.tile([P, PASSES * GROUP], U8, name="x_scales", align_bytes=256)
        v_codes = const.tile([P, PASSES * GROUP], U32, name="v_codes", align_bytes=256)
        v_scales = const.tile([P, PASSES * GROUP], U8, name="v_scales", align_bytes=256)

        q_bytes = {}
        row_tiles = {}
        needs_scale = {}
        turned = {}
        grouped = {}
        codes = {"x": x_codes, "v": v_codes}
        scales = {"x": x_scales, "v": v_scales}
        planes = {}
        sums = {}
        parts = {}

        free_banks = list(range(PSUM_BANKS))

        def take_bank():
            b = free_banks[0]
            free_banks.remove(b)
            t = psum.tile([P, GROUP], F32, name="bank%d" % b, tag="bank%d" % b)
            return (b, t)

        def load_bytes(j, r):
            t = bytes_pool.tile([P, K], U8, name="q_bytes", tag="q_bytes")
            row0 = GROUP * j + P * r
            nc.sync.dma_start(out=t[:], in_=q_w_bytes[row0 : row0 + P, :])
            q_bytes[(j, r)] = t

        def load_rows(grp, r):
            t = rows_pool.tile([P, K], BF16, name="rows", tag="rows")
            nc.sync.dma_start(out=t[:], in_=rows_of[grp][P * r : P * (r + 1), :])
            row_tiles[(grp, r)] = t
            needs_scale[(grp, r)] = False

        def load_scale_on_k(g):
            nc.sync.dma_start(
                out=scale_on_k[:, g, 0:PACK],
                in_=q_w_scale.rearrange("o (g p t) -> g p (o t)", p=P, t=PACK)[g],
            )

        def load_tables():
            cos_rows = cos.rearrange("b (t s) d -> s (b t) d", s=P)
            sin_rows = sin.rearrange("b (t s) d -> s (b t) d", s=P)
            for a in range(2):
                nc.sync.dma_start(out=rope_table[:, :, a, 0, :], in_=cos_rows[:, :, HALF * a : HALF * (a + 1)])
            nc.sync.dma_start(out=rope_table[:, :, 0, 1, :], in_=sin_rows[:, :, HALF:P])
            nc.sync.dma_start(out=low_sin[:], in_=sin_rows[:, :, 0:HALF])

        def negate_low_sin():
            nc.scalar.activation(out=rope_table[:, :, 1, 1, :], in_=low_sin[:], func=COPY, scale=-1.0)

        def spread_scale(g):
            b, bank = take_bank()
            for t in range(PACK):
                column = scale_on_k[:, g, t : t + 1]
                nc.tensor.transpose(bank[:, P * t : P * (t + 1)], column.to_broadcast([P, P]), ident[:])
            free_banks.append(b)
            nc.scalar.copy(
                out=scale_on_rows[:, PASS_K * g : PASS_K * (g + 1)].rearrange("p (n t) -> p n t", t=PACK),
                in_=bank[:].rearrange("p (t n) -> p n t", t=PACK),
            )

        def scale_rows(j, r, pieces=1):
            t = scaled_pool.tile([P, K], BF16, name="scaled", tag="scaled")
            width = K // pieces
            for c in range(pieces):
                cols = slice(width * c, width * (c + 1))
                nc.vector.tensor_tensor(
                    out=t[:, cols],
                    in0=q_bytes[(j, r)][:, cols].bitcast(FP8),
                    in1=scale_on_rows[:, cols],
                    op=MULT,
                )
            row_tiles[(j, r)] = t
            needs_scale[(j, r)] = False

        def widen_rows(j, r):
            t = widened_pool.tile([P, K], BF16, name="widened", tag="widened")
            nc.scalar.copy(out=t[:], in_=q_bytes[(j, r)][:].bitcast(FP8))
            row_tiles[(j, r)] = t
            needs_scale[(j, r)] = True

        def turn(grp, a, g):
            b, bank = take_bank()
            for u in range(2):
                for half_pair in range(2):
                    words = row_tiles[(grp, 2 * a + half_pair)][:].bitcast(F32)
                    c0 = (2 * u + half_pair) * P
                    nc.tensor.transpose(
                        bank[:, c0 : c0 + P], words[:, 256 * g + u : 256 * (g + 1) : 2], ident[:]
                    )
            turned[(grp, a, g)] = (b, bank)

        def grouped_slot(grp, a, g):
            if grp not in grouped:
                gt = grouped_pool.tile(
                    [P, PASSES * GROUP * PACK], BF16, name="grouped", tag="grouped", align_bytes=256
                )
                grouped[grp] = gt
            c0 = GROUP * PACK * g + 2 * P * PACK * a
            return grouped[grp][:, c0 : c0 + 2 * P * PACK]

        def scale_out(j, a, g):
            b, bank = turned[(j, a, g)]
            free_banks.append(b)
            pl = planes_pool.tile([P, PACK, 2 * P], BF16, name="planes", tag="planes")
            planes[(j, a, g)] = pl
            values = bank[:].bitcast(BF16).rearrange("p (u r e) -> p u r e", u=2, e=2)
            for t in range(PACK):
                nc.scalar.activation(
                    out=pl[:, t, :], in_=values[:, t // 2, :, t % 2], func=COPY, scale=scale_on_k[:, g, t : t + 1]
                )

        def interleave(engine_name, j, a, g):
            dst = grouped_slot(j, a, g).rearrange("p (c i t) -> p c t i", i=4, t=PACK)
            src = planes[(j, a, g)][:].rearrange("p t (c i) -> p c t i", i=4)
            if engine_name == "gpsimd":
                nc.gpsimd.tensor_scalar(out=dst, in0=src, scalar1=1.0, scalar2=0.0, op0=MULT, op1=ADD)
            else:
                nc.scalar.copy(out=dst, in_=src)

        def empty(grp, a, g):
            b, bank = turned[(grp, a, g)]
            free_banks.append(b)
            dst = grouped_slot(grp, a, g)
            if needs_scale[(grp, 2 * a)]:
                nc.vector.tensor_tensor(
                    out=dst.rearrange("p (r u e) -> p r u e", u=2, e=2),
                    in0=bank[:].bitcast(BF16).rearrange("p (u r e) -> p r u e", u=2, e=2),
                    in1=scale_on_k[:, g, 0:PACK]
                    .rearrange("p (o u e) -> p o u e", o=1, u=2)
                    .to_broadcast([P, 2 * P, 2, 2]),
                    op=MULT,
                )
            else:
                nc.scalar.copy(
                    out=dst.bitcast(F32).rearrange("p (r u) -> p r u", u=2),
                    in_=bank[:].rearrange("p (u r) -> p r u", u=2),
                )

        def turn_and_empty(grp, a, passes):
            for g in passes:
                turn(grp, a, g)
                empty(grp, a, g)

        def quantize(grp, h):
            if h == 0 and grp not in ("x", "v"):
                ct = codes_pool.tile([P, PASSES * GROUP], U32, name="codes", tag="codes", align_bytes=256)
                st = codes_pool.tile([P, PASSES * GROUP], U8, name="scales", tag="scales", align_bytes=256)
                codes[grp] = ct
                scales[grp] = st
            cols = slice(2 * GROUP * h, 2 * GROUP * (h + 1))
            nc.vector.quantize_mx(
                out=codes[grp][:, cols].bitcast(FP8X4),
                scales=scales[grp][:, cols],
                in_=grouped[grp][:, 2 * GROUP * PACK * h : 2 * GROUP * PACK * (h + 1)],
            )

        def project(grp, m, passes=(0, 1, 2, 3)):
            if passes[0] == 0:
                sums[(grp, m)] = take_bank()
            b, bank = sums[(grp, m)]
            for g in passes:
                x_cols = slice(GROUP * g + P * m, GROUP * g + P * (m + 1))
                w_cols = slice(GROUP * g, GROUP * (g + 1))
                nc.tensor.matmul_mx(
                    out=bank[:],
                    lhsT=x_codes[:, x_cols].bitcast(FP8X4),
                    lhsT_scale=x_scales[:, x_cols],
                    rhs=codes[grp][:, w_cols].bitcast(FP8X4),
                    rhs_scale=scales[grp][:, w_cols],
                    start=(g == 0),
                    stop=(g == PASSES - 1),
                )

        def quantize_and_project(grp):
            quantize(grp, 0)
            project(grp, 0, (0, 1))
            project(grp, 1, (0, 1))
            quantize(grp, 1)
            project(grp, 0, (2, 3))
            project(grp, 1, (2, 3))
            project(grp, 2)
            project(grp, 3)

        def dest(grp, m):
            batch = m // 2
            s0 = P * (m % 2)
            if grp == "k":
                o = out_1[batch, :, s0 : s0 + P, :]
            elif grp == "v":
                o = out_2[batch, :, s0 : s0 + P, :]
            else:
                o = out_0[batch, HEADS * grp : HEADS * (grp + 1), s0 : s0 + P, :]
            return o.rearrange("h s d -> s h d")

        def rope_products(grp, m):
            if m % 2 == 0:
                pt = parts_pool.tile([P, 4 * GROUP], F32, name="parts", tag="parts")
                parts[(grp, m // 2)] = pt
            cols = slice(2 * GROUP * (m % 2), 2 * GROUP * (m % 2 + 1))
            b, bank = sums[(grp, m)]
            free_banks.append(b)
            shape = [P, HEADS, 2, 2, HALF]
            nc.vector.tensor_tensor(
                out=parts[(grp, m // 2)][:, cols].rearrange("p (h a c j) -> p h a c j", h=HEADS, c=2, a=2),
                in0=bank[:].rearrange("p (h a o j) -> p h a o j", h=HEADS, a=2, o=1).to_broadcast(shape),
                in1=rope_table[:, m : m + 1, :, :, :].to_broadcast(shape),
                op=MULT,
            )

        def rope_sum(engine, grp, ms):
            pt = parts[(grp, ms[0] // 2)]
            cols = slice(2 * GROUP * (ms[0] % 2), 2 * GROUP * (ms[-1] % 2 + 1))
            blocks = pt[:, cols].rearrange("p (n q j) -> p n q j", q=4, j=HALF)
            engine.tensor_tensor(
                out=blocks[:, :, 0:2, :], in0=blocks[:, :, 0:4:2, :], in1=blocks[:, :, 3::-2, :], op=ADD
            )
            for m in ms:
                m_cols = slice(2 * GROUP * (m % 2), 2 * GROUP * (m % 2 + 1))
                nc.sync.dma_start(
                    out=dest(grp, m), in_=pt[:, m_cols].rearrange("p (h c d) -> p h c d", h=HEADS, c=2)[:, :, 0, :]
                )

        def rope_two(grp, m):
            for mm in (m, m + 1):
                rope_products(grp, mm)
                rope_sum(nc.gpsimd, grp, [mm])

        def store_plain(m):
            ot = plain_pool.tile([P, GROUP], F32, name="plain", tag="plain")
            b, bank = sums[("v", m)]
            free_banks.append(b)
            nc.scalar.copy(out=ot[:], in_=bank[:])
            nc.sync.dma_start(out=dest("v", m), in_=ot[:].rearrange("p (h d) -> p h d", h=HEADS))

        make_identity(nc, ident[:])
        load_scale_on_k(0)
        load_bytes(0, 0)
        for g in range(1, PASSES):
            load_scale_on_k(g)
        load_bytes(0, 1)
        load_rows("x", 0)
        load_rows("x", 1)
        load_bytes(0, 2)
        load_rows("x", 2)
        load_rows("x", 3)
        load_bytes(0, 3)
        load_bytes(1, 0)
        load_rows("v", 0)
        load_rows("v", 1)
        load_bytes(1, 1)
        load_rows("v", 2)
        load_rows("v", 3)
        for j, r in ((2, 0), (1, 2), (1, 3), (2, 1)):
            load_bytes(j, r)
        load_tables()
        for j, r in ((2, 2), (2, 3), (3, 0), (3, 1)):
            load_bytes(j, r)

        for g in range(PASSES):
            spread_scale(g)
        scale_rows(0, 0, pieces=PASSES)
        for r in range(1, 4):
            scale_rows(0, r)
        first = [(grp, a, g) for grp, a in (("x", 0), (0, 0), ("x", 1), ("v", 0), (0, 1), ("v", 1), (1, 0)) for g in range(PASSES)]
        for i in range(len(first) + TURNS_AHEAD):
            if i < len(first):
                turn(*first[i])
                if first[i] == (0, 0, PASSES - 1):
                    scale_rows(1, 0)
                    scale_rows(1, 1)
            if i >= TURNS_AHEAD:
                empty(*first[i - TURNS_AHEAD])
                if first[i - TURNS_AHEAD] == ("x", 1, PASSES - 1):
                    quantize("x", 0)
                    quantize("x", 1)
                if first[i - TURNS_AHEAD] == (0, 1, PASSES - 1):
                    quantize(0, 0)
                if first[i - TURNS_AHEAD] == ("v", 1, PASSES - 1):
                    quantize("v", 0)
                    quantize("v", 1)
        for r in range(4):
            load_rows("k", r)
        load_bytes(3, 2)
        load_bytes(3, 3)
        negate_low_sin()
        widen_rows(1, 2)
        widen_rows(1, 3)
        project(0, 0, (0, 1))
        project(0, 1, (0, 1))
        for m in (0, 1):
            project("v", m)
            store_plain(m)
        quantize(0, 1)
        project(0, 0, (2, 3))
        project(0, 1, (2, 3))
        project(0, 2)
        turn(1, 1, 2)
        turn(1, 1, 3)
        project(0, 3)
        turn(1, 1, 0)
        turn(1, 1, 1)
        scale_rows(2, 0)
        scale_rows(2, 1)
        widen_rows(2, 3)
        widen_rows(2, 2)
        scale_out(1, 1, 2)
        scale_out(1, 1, 3)
        interleave("scalar", 1, 1, 2)
        interleave("scalar", 1, 1, 3)

        rope_two(0, 0)
        rope_two(0, 2)
        empty(1, 1, 0)
        empty(1, 1, 1)
        turn(2, 0, 0)
        turn(2, 0, 1)
        empty(2, 0, 0)
        empty(2, 0, 1)
        turn(2, 1, 1)
        turn(2, 0, 2)
        turn(2, 0, 3)
        scale_out(2, 1, 1)
        empty(2, 0, 2)
        empty(2, 0, 3)
        interleave("scalar", 2, 1, 1)
        turn(2, 1, 0)
        turn_and_empty("k", 0, range(PASSES))
        widen_rows(3, 0)
        widen_rows(3, 1)
        quantize_and_project(1)

        empty(2, 1, 0)
        rope_two(1, 0)
        turn(2, 1, 2)
        rope_products(1, 2)
        rope_sum(nc.gpsimd, 1, [2])
        turn(2, 1, 3)
        rope_products(1, 3)
        rope_sum(nc.gpsimd, 1, [3])
        turn_and_empty("k", 1, range(PASSES))
        widen_rows(3, 2)
        empty(2, 1, 2)
        turn(3, 0, 0)
        empty(2, 1, 3)
        turn(3, 0, 1)
        scale_out(3, 0, 1)
        interleave("scalar", 3, 0, 1)
        turn(3, 0, 2)
        widen_rows(3, 3)
        quantize_and_project(2)
        empty(3, 0, 0)
        quantize("k", 0)
        quantize("k", 1)

        rope_two(2, 0)
        scale_out(3, 0, 2)
        turn(3, 0, 3)
        scale_out(3, 0, 3)
        rope_two(2, 2)
        turn(3, 1, 2)
        interleave("scalar", 3, 0, 2)
        project("k", 0)
        turn(3, 1, 3)
        interleave("scalar", 3, 0, 3)
        turn(3, 1, 0)
        scale_out(3, 1, 2)
        turn(3, 1, 1)
        scale_out(3, 1, 3)
        project("k", 1)
        interleave("scalar", 3, 1, 2)
        interleave("scalar", 3, 1, 3)
        project("k", 2)
        project("k", 3)

        rope_products("k", 0)
        rope_sum(nc.gpsimd, "k", [0])
        empty(3, 1, 0)
        empty(3, 1, 1)
        rope_products("k", 1)
        rope_sum(nc.gpsimd, "k", [1])
        project("v", 2)
        project("v", 3)
        store_plain(2)
        store_plain(3)
        quantize(3, 0)
        project(3, 0, (0, 1))
        project(3, 1, (0, 1))
        rope_products("k", 2)
        rope_sum(nc.gpsimd, "k", [2])
        quantize(3, 1)
        project(3, 0, (2, 3))
        project(3, 1, (2, 3))
        project(3, 2)
        project(3, 3)

        rope_products("k", 3)
        rope_sum(nc.gpsimd, "k", [3])
        rope_two(3, 0)
        rope_products(3, 2)
        rope_products(3, 3)
        rope_sum(nc.vector, 3, [2])
        rope_sum(nc.vector, 3, [3])
